import numpy as np
import ml_dtypes


def mxq(x, axis, fmt="e4m3"):
    dtype, down = {"e4m3": (ml_dtypes.float8_e4m3fn, 7), "e5m2": (ml_dtypes.float8_e5m2, 14)}[fmt]
    v = np.moveaxis(np.asarray(x, np.float32).astype(ml_dtypes.bfloat16).astype(np.float64), axis, -1)
    blocks = v.reshape(v.shape[:-1] + (-1, 32))
    amax = np.abs(blocks).max(-1, keepdims=True)
    byte = np.maximum(np.where(amax > 0, np.frexp(amax)[1] - 1 + 127, 0) - down, 1)
    scale = np.exp2(byte - 127.0)
    codes = (blocks / scale).astype(np.float32).astype(dtype).astype(np.float64)
    return np.moveaxis((codes * scale).reshape(v.shape), -1, axis)


WIDE = False


def mx_kscale(k):
    if not WIDE:
        return np.ones(k)
    levels = np.array([10, -10, 5, -5, 0])
    a = np.random.permutation(np.resize(levels, k // 512 * 4)).reshape(k // 512, 4)
    idx = np.arange(k)
    return np.exp2(a[idx // 512, idx % 128 // 32])


BF16 = ml_dtypes.bfloat16


def bf(x):
    return np.asarray(x, np.float32).astype(BF16)


def f64(x):
    return np.asarray(x).astype(np.float64)


B, MI, MO, NL = 384, 512, 1024, 4
IR_DIMS = tuple(2 * l + 1 for l in range(NL))
FLAT_IN = MI * sum(IR_DIMS)


def setup_inputs():
    s = mx_kscale(MI)
    sx = np.concatenate([np.repeat(s, d) for d in IR_DIMS])
    inp = {"x": bf(np.random.standard_normal((B, FLAT_IN)) * sx)}
    for l in range(NL):
        inp["W%d" % l] = bf(np.random.standard_normal((MO, MI)) / np.sqrt(MI) / s[None, :])
    inp["bias"] = bf(np.random.standard_normal(MO))
    return inp


def reference(x, W0, W1, W2, W3, bias):
    x = f64(x)
    outs = []
    start = 0
    for d, W in zip(IR_DIMS, (W0, W1, W2, W3)):
        seg = x[:, start:start + MI * d].reshape(B, MI, d)
        rows = seg.transpose(0, 2, 1).reshape(B * d, MI)
        y = mxq(rows, 1, "e4m3") @ mxq(f64(W).T, 0, "e4m3")
        outs.append(y.reshape(B, d, MO).transpose(0, 2, 1).reshape(B, MO * d))
        start += MI * d
    outs[0] = outs[0] + f64(bias)
    return np.concatenate(outs, axis=1)

@@ -1,0 +1,203 @@
+from contextlib import ExitStack
+
+import concourse.mybir as mybir
+from concourse.masks import make_identity
+
+F32 = mybir.dt.float32
+BF16 = mybir.dt.bfloat16
+U32 = mybir.dt.uint32
+U8 = mybir.dt.uint8
+FP8X4 = mybir.dt.float8_e4m3fn_x4
+
+P = 128
+BATCH = 384
+B_TILES = BATCH // P
+C_IN = 512
+C_OUT = 1024
+WORDS = C_IN // 2
+BANK = 512
+DEGREES = (3, 2, 1, 0)
+UNITS = [(l, i) for l in DEGREES for i in range(2 * l + 1)]
+GROUP = 4
+W_HALF = GROUP * P
+CHUNK_BANKS = 4
+HEAD = 3
+
+FLOPS = 2 * BATCH * len(UNITS) * C_IN * C_OUT
+
+
+def pass_width(d):
+    return max(n for n in (64, 128, 256, 512) if n * d <= BANK)
+
+
+def first_unit(l):
+    return UNITS.index((l, 0))
+
+
+def operand_groups():
+    groups = []
+    for bt in range(B_TILES):
+        listed = 0
+        for l in DEGREES:
+            last_group = (first_unit(l) + 2 * l) // GROUP
+            while listed <= last_group:
+                groups.append(("x", bt, listed))
+                listed += 1
+            if bt == 0:
+                groups.append(("w", l, 0))
+                groups.append(("w", l, 1))
+    return groups
+
+
+def tile_so3_linear_pa_t_kernel(tc, x, W0, W1, W2, W3, bias, out):
+    nc = tc.nc
+    weights = (W0, W1, W2, W3)
+
+    with ExitStack() as ctx:
+        keep = ctx.enter_context(tc.tile_pool(name="keep", bufs=1))
+        gathered_pool = ctx.enter_context(tc.tile_pool(name="gathered", bufs=3))
+        regrouped_pool = ctx.enter_context(tc.tile_pool(name="regrouped", bufs=3))
+        staged_pool = ctx.enter_context(tc.tile_pool(name="staged", bufs=8))
+        flipped_pool = ctx.enter_context(tc.psum_pool(name="flipped", bufs=3))
+        product_pool = ctx.enter_context(tc.psum_pool(name="product", bufs=5))
+
+        identity = keep.tile([P, P], F32, name="identity")
+        make_identity(nc, identity[:])
+
+        x_raw = []
+        for bt in range(B_TILES):
+            x_raw.append(keep.tile([P, x.shape[1]], BF16, name="x_raw%d" % bt))
+        w_raw = {}
+        for l in DEGREES:
+            w_raw[l] = keep.tile([P, 2 * GROUP * C_IN], BF16, name="w_raw%d" % l)
+
+        def load_x(bt):
+            for l in DEGREES:
+                columns = slice(C_IN * l * l, C_IN * (l + 1) * (l + 1))
+                nc.sync.dma_start(out=x_raw[bt][:, columns], in_=x[bt * P : (bt + 1) * P, columns])
+
+        load_x(0)
+        for l in DEGREES:
+            for half in range(2):
+                nc.sync.dma_start(
+                    out=w_raw[l][:, half * GROUP * C_IN : (half + 1) * GROUP * C_IN].rearrange(
+                        "p (t m) -> p t m", t=GROUP
+                    ),
+                    in_=weights[l][half * W_HALF : (half + 1) * W_HALF, :].rearrange("(t p) m -> p t m", p=P),
+                )
+        load_x(1)
+        load_x(2)
+        bias_bf16 = keep.tile([P, C_OUT], BF16, name="bias_bf16")
+        nc.sync.dma_start(out=bias_bf16[:], in_=bias.partition_broadcast(P))
+        bias_f32 = keep.tile([P, C_OUT], F32, name="bias_f32")
+        nc.vector.tensor_copy(out=bias_f32[:], in_=bias_bf16[:])
+
+        x_codes, x_scales = [], []
+        for bt in range(B_TILES):
+            x_codes.append(keep.tile([P, len(UNITS) * P], U32, name="x_codes%d" % bt, align_bytes=64))
+            x_scales.append(keep.tile([P, len(UNITS) * P], U8, name="x_scales%d" % bt, align_bytes=64))
+        w_codes, w_scales = {}, {}
+        for l in DEGREES:
+            w_codes[l] = keep.tile([P, C_OUT], U32, name="w_codes%d" % l, align_bytes=64)
+            w_scales[l] = keep.tile([P, C_OUT], U8, name="w_scales%d" % l, align_bytes=64)
+
+        groups = operand_groups()
+        source_words = {}
+        regrouped = {}
+        quantised = set()
+
+        def gather(group):
+            kind, a, b = group
+            if kind == "w":
+                source_words[group] = w_raw[a][:].bitcast(F32)[:, b * GROUP * WORDS : (b + 1) * GROUP * WORDS]
+                return
+            rows = gathered_pool.tile([P, GROUP * C_IN], BF16, name="rows")
+            for j in range(GROUP):
+                l, i = UNITS[b * GROUP + j]
+                segment = x_raw[a][:, C_IN * l * l : C_IN * (l + 1) * (l + 1)]
+                nc.vector.tensor_copy(
+                    out=rows[:, j * C_IN : (j + 1) * C_IN],
+                    in_=segment.rearrange("p (m i) -> p i m", i=2 * l + 1)[:, i, :],
+                )
+            source_words[group] = rows[:].bitcast(F32)
+
+        def flip(group):
+            words = source_words[group]
+            packed = regrouped_pool.tile([P, GROUP * P * 4], BF16, name="packed", align_bytes=64)
+            packed_words = packed[:].bitcast(F32).rearrange("p (j r u) -> p j r u", j=GROUP, u=2)
+            for pair in range(GROUP // 2):
+                flipped = flipped_pool.tile([P, 2, 2, P], F32, name="flipped")
+                for j in range(2):
+                    for u in range(2):
+                        start = ((2 * pair + j) * 2 + u) * P
+                        nc.tensor.transpose(flipped[:, j, u, :], words[:, start : start + P], identity[:])
+                nc.scalar.copy(
+                    out=packed_words[:, 2 * pair : 2 * pair + 2, :, :],
+                    in_=flipped[:].rearrange("p j u r -> p j r u"),
+                )
+            regrouped[group] = packed
+
+        def quantise(group):
+            kind, a, b = group
+            codes, scales = (w_codes[a], w_scales[a]) if kind == "w" else (x_codes[a], x_scales[a])
+            columns = slice(b * GROUP * P, (b + 1) * GROUP * P)
+            nc.vector.quantize_mx(
+                out=codes[:, columns].bitcast(FP8X4), scales=scales[:, columns], in_=regrouped[group][:]
+            )
+            quantised.add(group)
+
+        def advance(step):
+            for stage, index in ((quantise, step), (flip, step + 1), (gather, step + 2)):
+                if 0 <= index < len(groups):
+                    stage(groups[index])
+
+        def chunk(bt, l, first_bank, banks):
+            d = 2 * l + 1
+            width = pass_width(d)
+            staged = staged_pool.tile([P, CHUNK_BANKS * BANK], F32, name="staged")
+            for k in range(banks):
+                n0 = (first_bank + k) * width
+                assert ("w", l, n0 // W_HALF) in quantised
+                product = product_pool.tile([P, d, width], F32, name="product")
+                for i in range(d):
+                    unit = first_unit(l) + i
+                    assert ("x", bt, unit // GROUP) in quantised
+                    nc.tensor.matmul_mx(
+                        out=product[:, i, :],
+                        lhsT=x_codes[bt][:, unit * P : (unit + 1) * P].bitcast(FP8X4),
+                        lhsT_scale=x_scales[bt][:, unit * P : (unit + 1) * P],
+                        rhs=w_codes[l][:, n0 : n0 + width].bitcast(FP8X4),
+                        rhs_scale=w_scales[l][:, n0 : n0 + width],
+                        start=True,
+                        stop=True,
+                    )
+                target = staged[:, k * width * d : (k + 1) * width * d]
+                if l == 0:
+                    nc.vector.tensor_tensor(
+                        out=target, in0=product[:, 0, :], in1=bias_f32[:, n0 : n0 + width], op=mybir.AluOpType.add
+                    )
+                elif k % 2 == 0:
+                    nc.vector.tensor_copy(
+                        out=target.rearrange("p (n i) -> p n i", i=d), in_=product[:].rearrange("p i n -> p n i")
+                    )
+                else:
+                    nc.scalar.copy(
+                        out=target.rearrange("p (n i) -> p n i", i=d), in_=product[:].rearrange("p i n -> p n i")
+                    )
+            start = C_OUT * l * l + first_bank * width * d
+            nc.sync.dma_start(
+                out=out[bt * P : (bt + 1) * P, start : start + banks * width * d],
+                in_=staged[:, : banks * width * d],
+            )
+
+        for step in range(-2, HEAD):
+            advance(step)
+        step = HEAD
+        for bt in range(B_TILES):
+            for l in DEGREES:
+                all_banks = C_OUT // pass_width(2 * l + 1)
+                banks = min(CHUNK_BANKS, all_banks)
+                for first_bank in range(0, all_banks, banks):
+                    chunk(bt, l, first_bank, banks)
+                    advance(step)
+                    step += 1

@@ -16,12 +16,11 @@ C_IN = 512
 C_OUT = 1024
 WORDS = C_IN // 2
 BANK = 512
-DEGREES = (3, 2, 1, 0)
+DEGREES = (1, 2, 0, 3)
 UNITS = [(l, i) for l in DEGREES for i in range(2 * l + 1)]
 GROUP = 4
 W_HALF = GROUP * P
 CHUNK_BANKS = 4
-HEAD = 3
 
 FLOPS = 2 * BATCH * len(UNITS) * C_IN * C_OUT
 
@@ -71,26 +70,24 @@ def tile_so3_linear_pa_t_kernel(tc, x, W0, W1, W2, W3, bias, out):
         for l in DEGREES:
             w_raw[l] = keep.tile([P, 2 * GROUP * C_IN], BF16, name="w_raw%d" % l)
 
-        def load_x(bt):
-            for l in DEGREES:
-                columns = slice(C_IN * l * l, C_IN * (l + 1) * (l + 1))
-                nc.sync.dma_start(out=x_raw[bt][:, columns], in_=x[bt * P : (bt + 1) * P, columns])
-
-        load_x(0)
-        for l in DEGREES:
-            for half in range(2):
-                nc.sync.dma_start(
-                    out=w_raw[l][:, half * GROUP * C_IN : (half + 1) * GROUP * C_IN].rearrange(
-                        "p (t m) -> p t m", t=GROUP
-                    ),
-                    in_=weights[l][half * W_HALF : (half + 1) * W_HALF, :].rearrange("(t p) m -> p t m", p=P),
-                )
-        load_x(1)
-        load_x(2)
         bias_bf16 = keep.tile([P, C_OUT], BF16, name="bias_bf16")
-        nc.sync.dma_start(out=bias_bf16[:], in_=bias.partition_broadcast(P))
+        groups = operand_groups()
+        loaded = set()
+        for kind, a, b in groups:
+            if kind == "w":
+                nc.sync.dma_start(
+                    out=w_raw[a][:, b * GROUP * C_IN : (b + 1) * GROUP * C_IN].rearrange("p (t m) -> p t m", t=GROUP),
+                    in_=weights[a][b * W_HALF : (b + 1) * W_HALF, :].rearrange("(t p) m -> p t m", p=P),
+                )
+                if (a, b) == (0, 0):
+                    nc.sync.dma_start(out=bias_bf16[:], in_=bias.partition_broadcast(P))
+            else:
+                for l, i in UNITS[b * GROUP : (b + 1) * GROUP]:
+                    if (a, l) not in loaded:
+                        loaded.add((a, l))
+                        columns = slice(C_IN * l * l, C_IN * (l + 1) * (l + 1))
+                        nc.sync.dma_start(out=x_raw[a][:, columns], in_=x[a * P : (a + 1) * P, columns])
         bias_f32 = keep.tile([P, C_OUT], F32, name="bias_f32")
-        nc.vector.tensor_copy(out=bias_f32[:], in_=bias_bf16[:])
 
         x_codes, x_scales = [], []
         for bt in range(B_TILES):
@@ -101,7 +98,6 @@ def tile_so3_linear_pa_t_kernel(tc, x, W0, W1, W2, W3, bias, out):
             w_codes[l] = keep.tile([P, C_OUT], U32, name="w_codes%d" % l, align_bytes=64)
             w_scales[l] = keep.tile([P, C_OUT], U8, name="w_scales%d" % l, align_bytes=64)
 
-        groups = operand_groups()
         source_words = {}
         regrouped = {}
         quantised = set()
@@ -110,6 +106,8 @@ def tile_so3_linear_pa_t_kernel(tc, x, W0, W1, W2, W3, bias, out):
             kind, a, b = group
             if kind == "w":
                 source_words[group] = w_raw[a][:].bitcast(F32)[:, b * GROUP * WORDS : (b + 1) * GROUP * WORDS]
+                if (a, b) == (0, 0):
+                    nc.vector.tensor_copy(out=bias_f32[:], in_=bias_bf16[:])
                 return
             rows = gathered_pool.tile([P, GROUP * C_IN], BF16, name="rows")
             for j in range(GROUP):
@@ -151,17 +149,21 @@ def tile_so3_linear_pa_t_kernel(tc, x, W0, W1, W2, W3, bias, out):
                 if 0 <= index < len(groups):
                     stage(groups[index])
 
+        def operands(bt, l, first_bank, banks):
+            width = pass_width(2 * l + 1)
+            halves = [("w", l, (first_bank + k) * width // W_HALF) for k in range(banks)]
+            return halves + [("x", bt, (first_unit(l) + i) // GROUP) for i in range(2 * l + 1)]
+
         def chunk(bt, l, first_bank, banks):
+            assert all(group in quantised for group in operands(bt, l, first_bank, banks))
             d = 2 * l + 1
             width = pass_width(d)
             staged = staged_pool.tile([P, CHUNK_BANKS * BANK], F32, name="staged")
             for k in range(banks):
                 n0 = (first_bank + k) * width
-                assert ("w", l, n0 // W_HALF) in quantised
                 product = product_pool.tile([P, d, width], F32, name="product")
                 for i in range(d):
                     unit = first_unit(l) + i
-                    assert ("x", bt, unit // GROUP) in quantised
                     nc.tensor.matmul_mx(
                         out=product[:, i, :],
                         lhsT=x_codes[bt][:, unit * P : (unit + 1) * P].bitcast(FP8X4),
@@ -190,14 +192,21 @@ def tile_so3_linear_pa_t_kernel(tc, x, W0, W1, W2, W3, bias, out):
                 in_=staged[:, : banks * width * d],
             )
 
-        for step in range(-2, HEAD):
-            advance(step)
-        step = HEAD
+        chunks = []
         for bt in range(B_TILES):
             for l in DEGREES:
                 all_banks = C_OUT // pass_width(2 * l + 1)
                 banks = min(CHUNK_BANKS, all_banks)
                 for first_bank in range(0, all_banks, banks):
-                    chunk(bt, l, first_bank, banks)
-                    advance(step)
-                    step += 1
+                    chunks.append((bt, l, first_bank, banks))
+
+        step = -2
+        for q in range(-1, len(chunks)):
+            if q >= 0:
+                chunk(*chunks[q])
+                advance(step)
+                step += 1
+            ahead = chunks[min(q + 2, len(chunks) - 1)]
+            while not all(group in quantised for group in operands(*ahead)):
+                advance(step)
+                step += 1

@@ -16,11 +16,12 @@ C_IN = 512
 C_OUT = 1024
 WORDS = C_IN // 2
 BANK = 512
-DEGREES = (1, 2, 0, 3)
+DEGREES = (1, 0, 3, 2)
 UNITS = [(l, i) for l in DEGREES for i in range(2 * l + 1)]
 GROUP = 4
 W_HALF = GROUP * P
 CHUNK_BANKS = 4
+LOAD_LEAD = 6
 
 FLOPS = 2 * BATCH * len(UNITS) * C_IN * C_OUT
 
@@ -48,6 +49,23 @@ def operand_groups():
     return groups
 
 
+def product_chunks():
+    chunks = []
+    for bt in range(B_TILES):
+        for l in DEGREES:
+            all_banks = C_OUT // pass_width(2 * l + 1)
+            banks = min(CHUNK_BANKS, all_banks)
+            for first_bank in range(0, all_banks, banks):
+                chunks.append((bt, l, first_bank, banks))
+    return chunks
+
+
+def operands(bt, l, first_bank, banks):
+    width = pass_width(2 * l + 1)
+    halves = [("w", l, (first_bank + k) * width // W_HALF) for k in range(banks)]
+    return halves + [("x", bt, (first_unit(l) + i) // GROUP) for i in range(2 * l + 1)]
+
+
 def tile_so3_linear_pa_t_kernel(tc, x, W0, W1, W2, W3, bias, out):
     nc = tc.nc
     weights = (W0, W1, W2, W3)
@@ -59,6 +77,7 @@ def tile_so3_linear_pa_t_kernel(tc, x, W0, W1, W2, W3, bias, out):
         staged_pool = ctx.enter_context(tc.tile_pool(name="staged", bufs=8))
         flipped_pool = ctx.enter_context(tc.psum_pool(name="flipped", bufs=3))
         product_pool = ctx.enter_context(tc.psum_pool(name="product", bufs=5))
+        ctx.enter_context(tc.manual_schedule())
 
         identity = keep.tile([P, P], F32, name="identity")
         make_identity(nc, identity[:])
@@ -69,24 +88,7 @@ def tile_so3_linear_pa_t_kernel(tc, x, W0, W1, W2, W3, bias, out):
         w_raw = {}
         for l in DEGREES:
             w_raw[l] = keep.tile([P, 2 * GROUP * C_IN], BF16, name="w_raw%d" % l)
-
         bias_bf16 = keep.tile([P, C_OUT], BF16, name="bias_bf16")
-        groups = operand_groups()
-        loaded = set()
-        for kind, a, b in groups:
-            if kind == "w":
-                nc.sync.dma_start(
-                    out=w_raw[a][:, b * GROUP * C_IN : (b + 1) * GROUP * C_IN].rearrange("p (t m) -> p t m", t=GROUP),
-                    in_=weights[a][b * W_HALF : (b + 1) * W_HALF, :].rearrange("(t p) m -> p t m", p=P),
-                )
-                if (a, b) == (0, 0):
-                    nc.sync.dma_start(out=bias_bf16[:], in_=bias.partition_broadcast(P))
-            else:
-                for l, i in UNITS[b * GROUP : (b + 1) * GROUP]:
-                    if (a, l) not in loaded:
-                        loaded.add((a, l))
-                        columns = slice(C_IN * l * l, C_IN * (l + 1) * (l + 1))
-                        nc.sync.dma_start(out=x_raw[a][:, columns], in_=x[a * P : (a + 1) * P, columns])
         bias_f32 = keep.tile([P, C_OUT], F32, name="bias_f32")
 
         x_codes, x_scales = [], []
@@ -98,9 +100,27 @@ def tile_so3_linear_pa_t_kernel(tc, x, W0, W1, W2, W3, bias, out):
             w_codes[l] = keep.tile([P, C_OUT], U32, name="w_codes%d" % l, align_bytes=64)
             w_scales[l] = keep.tile([P, C_OUT], U8, name="w_scales%d" % l, align_bytes=64)
 
+        groups = operand_groups()
+        loaded = set()
         source_words = {}
         regrouped = {}
         quantised = set()
+
+        def load(group):
+            kind, a, b = group
+            if kind == "w":
+                nc.sync.dma_start(
+                    out=w_raw[a][:, b * GROUP * C_IN : (b + 1) * GROUP * C_IN].rearrange("p (t m) -> p t m", t=GROUP),
+                    in_=weights[a][b * W_HALF : (b + 1) * W_HALF, :].rearrange("(t p) m -> p t m", p=P),
+                )
+                if (a, b) == (0, 0):
+                    nc.sync.dma_start(out=bias_bf16[:], in_=bias.partition_broadcast(P))
+                return
+            for l, i in UNITS[b * GROUP : (b + 1) * GROUP]:
+                if (a, l) not in loaded:
+                    loaded.add((a, l))
+                    columns = slice(C_IN * l * l, C_IN * (l + 1) * (l + 1))
+                    nc.sync.dma_start(out=x_raw[a][:, columns], in_=x[a * P : (a + 1) * P, columns])
 
         def gather(group):
             kind, a, b = group
@@ -145,14 +165,9 @@ def tile_so3_linear_pa_t_kernel(tc, x, W0, W1, W2, W3, bias, out):
             quantised.add(group)
 
         def advance(step):
-            for stage, index in ((quantise, step), (flip, step + 1), (gather, step + 2)):
+            for stage, index in ((quantise, step), (gather, step + 2), (flip, step + 1), (load, step + LOAD_LEAD)):
                 if 0 <= index < len(groups):
                     stage(groups[index])
-
-        def operands(bt, l, first_bank, banks):
-            width = pass_width(2 * l + 1)
-            halves = [("w", l, (first_bank + k) * width // W_HALF) for k in range(banks)]
-            return halves + [("x", bt, (first_unit(l) + i) // GROUP) for i in range(2 * l + 1)]
 
         def chunk(bt, l, first_bank, banks):
             assert all(group in quantised for group in operands(bt, l, first_bank, banks))
@@ -178,7 +193,7 @@ def tile_so3_linear_pa_t_kernel(tc, x, W0, W1, W2, W3, bias, out):
                     nc.vector.tensor_tensor(
                         out=target, in0=product[:, 0, :], in1=bias_f32[:, n0 : n0 + width], op=mybir.AluOpType.add
                     )
-                elif k % 2 == 0:
+                elif k == 0:
                     nc.vector.tensor_copy(
                         out=target.rearrange("p (n i) -> p n i", i=d), in_=product[:].rearrange("p i n -> p n i")
                     )
@@ -192,15 +207,8 @@ def tile_so3_linear_pa_t_kernel(tc, x, W0, W1, W2, W3, bias, out):
                 in_=staged[:, : banks * width * d],
             )
 
-        chunks = []
-        for bt in range(B_TILES):
-            for l in DEGREES:
-                all_banks = C_OUT // pass_width(2 * l + 1)
-                banks = min(CHUNK_BANKS, all_banks)
-                for first_bank in range(0, all_banks, banks):
-                    chunks.append((bt, l, first_bank, banks))
-
-        step = -2
+        chunks = product_chunks()
+        step = -LOAD_LEAD
         for q in range(-1, len(chunks)):
             if q >= 0:
                 chunk(*chunks[q])

@@ -7,6 +7,7 @@ F32 = mybir.dt.float32
 BF16 = mybir.dt.bfloat16
 U32 = mybir.dt.uint32
 U8 = mybir.dt.uint8
+I32 = mybir.dt.int32
 FP8X4 = mybir.dt.float8_e4m3fn_x4
 
 P = 128
@@ -22,6 +23,7 @@ GROUP = 4
 W_HALF = GROUP * P
 CHUNK_BANKS = 4
 LOAD_LEAD = 6
+MIN_MOVING = 128
 
 FLOPS = 2 * BATCH * len(UNITS) * C_IN * C_OUT
 
@@ -97,8 +99,10 @@ def tile_so3_linear_pa_t_kernel(tc, x, W0, W1, W2, W3, bias, out):
             x_scales.append(keep.tile([P, len(UNITS) * P], U8, name="x_scales%d" % bt, align_bytes=64))
         w_codes, w_scales = {}, {}
         for l in DEGREES:
-            w_codes[l] = keep.tile([P, C_OUT], U32, name="w_codes%d" % l, align_bytes=64)
-            w_scales[l] = keep.tile([P, C_OUT], U8, name="w_scales%d" % l, align_bytes=64)
+            w_codes[l] = keep.tile([P, C_OUT + MIN_MOVING // 2], U32, name="w_codes%d" % l, align_bytes=64)
+            w_scales[l] = keep.tile([P, C_OUT + MIN_MOVING // 2], U8, name="w_scales%d" % l, align_bytes=64)
+            nc.vector.memset(w_codes[l][:, C_OUT:].bitcast(I32), 0)
+            nc.vector.memset(w_scales[l][:, C_OUT:].bitcast(I32), 0)
 
         groups = operand_groups()
         loaded = set()
@@ -173,33 +177,34 @@ def tile_so3_linear_pa_t_kernel(tc, x, W0, W1, W2, W3, bias, out):
             assert all(group in quantised for group in operands(bt, l, first_bank, banks))
             d = 2 * l + 1
             width = pass_width(d)
+            moving = max(width, MIN_MOVING)
             staged = staged_pool.tile([P, CHUNK_BANKS * BANK], F32, name="staged")
             for k in range(banks):
                 n0 = (first_bank + k) * width
-                product = product_pool.tile([P, d, width], F32, name="product")
+                product = product_pool.tile([P, BANK], F32, name="product")
                 for i in range(d):
                     unit = first_unit(l) + i
                     nc.tensor.matmul_mx(
-                        out=product[:, i, :],
+                        out=product[:, i * width : i * width + moving],
                         lhsT=x_codes[bt][:, unit * P : (unit + 1) * P].bitcast(FP8X4),
                         lhsT_scale=x_scales[bt][:, unit * P : (unit + 1) * P],
-                        rhs=w_codes[l][:, n0 : n0 + width].bitcast(FP8X4),
-                        rhs_scale=w_scales[l][:, n0 : n0 + width],
+                        rhs=w_codes[l][:, n0 : n0 + moving].bitcast(FP8X4),
+                        rhs_scale=w_scales[l][:, n0 : n0 + moving],
                         start=True,
                         stop=True,
                     )
                 target = staged[:, k * width * d : (k + 1) * width * d]
                 if l == 0:
                     nc.vector.tensor_tensor(
-                        out=target, in0=product[:, 0, :], in1=bias_f32[:, n0 : n0 + width], op=mybir.AluOpType.add
+                        out=target, in0=product[:], in1=bias_f32[:, n0 : n0 + width], op=mybir.AluOpType.add
                     )
                 elif k == 0:
                     nc.vector.tensor_copy(
-                        out=target.rearrange("p (n i) -> p n i", i=d), in_=product[:].rearrange("p i n -> p n i")
+                        out=target.rearrange("p (n i) -> p n i", i=d), in_=product[:, : d * width].rearrange("p (i n) -> p n i", i=d)
                     )
                 else:
                     nc.scalar.copy(
-                        out=target.rearrange("p (n i) -> p n i", i=d), in_=product[:].rearrange("p i n -> p n i")
+                        out=target.rearrange("p (n i) -> p n i", i=d), in_=product[:, : d * width].rearrange("p (i n) -> p n i", i=d)
                     )
             start = C_OUT * l * l + first_bank * width * d
             nc.sync.dma_start(

@@ -7,7 +7,6 @@ F32 = mybir.dt.float32
 BF16 = mybir.dt.bfloat16
 U32 = mybir.dt.uint32
 U8 = mybir.dt.uint8
-I32 = mybir.dt.int32
 FP8X4 = mybir.dt.float8_e4m3fn_x4
 
 P = 128
@@ -22,8 +21,6 @@ UNITS = [(l, i) for l in DEGREES for i in range(2 * l + 1)]
 GROUP = 4
 W_HALF = GROUP * P
 CHUNK_BANKS = 4
-LOAD_LEAD = 6
-MIN_MOVING = 128
 
 FLOPS = 2 * BATCH * len(UNITS) * C_IN * C_OUT
 
@@ -90,8 +87,21 @@ def tile_so3_linear_pa_t_kernel(tc, x, W0, W1, W2, W3, bias, out):
         w_raw = {}
         for l in DEGREES:
             w_raw[l] = keep.tile([P, 2 * GROUP * C_IN], BF16, name="w_raw%d" % l)
-        bias_bf16 = keep.tile([P, C_OUT], BF16, name="bias_bf16")
+
+        bias_row = keep.tile([P, C_OUT], BF16, name="bias_row")
+        ones = keep.tile([P, P], BF16, name="ones")
         bias_f32 = keep.tile([P, C_OUT], F32, name="bias_f32")
+        nc.vector.memset(bias_row[:], 0.0)
+        nc.vector.memset(ones[:], 1.0)
+        nc.scalar.dma_start(out=bias_row[0:1, :], in_=bias.unsqueeze(0))
+
+        def spread_bias():
+            for half in range(C_OUT // BANK):
+                spread = product_pool.tile([P, BANK], F32, name="product")
+                nc.tensor.matmul(
+                    out=spread[:], lhsT=ones[:], rhs=bias_row[:, half * BANK : (half + 1) * BANK], start=True, stop=True
+                )
+                nc.scalar.copy(out=bias_f32[:, half * BANK : (half + 1) * BANK], in_=spread[:])
 
         x_codes, x_scales = [], []
         for bt in range(B_TILES):
@@ -99,10 +109,8 @@ def tile_so3_linear_pa_t_kernel(tc, x, W0, W1, W2, W3, bias, out):
             x_scales.append(keep.tile([P, len(UNITS) * P], U8, name="x_scales%d" % bt, align_bytes=64))
         w_codes, w_scales = {}, {}
         for l in DEGREES:
-            w_codes[l] = keep.tile([P, C_OUT + MIN_MOVING // 2], U32, name="w_codes%d" % l, align_bytes=64)
-            w_scales[l] = keep.tile([P, C_OUT + MIN_MOVING // 2], U8, name="w_scales%d" % l, align_bytes=64)
-            nc.vector.memset(w_codes[l][:, C_OUT:].bitcast(I32), 0)
-            nc.vector.memset(w_scales[l][:, C_OUT:].bitcast(I32), 0)
+            w_codes[l] = keep.tile([P, C_OUT], U32, name="w_codes%d" % l, align_bytes=64)
+            w_scales[l] = keep.tile([P, C_OUT], U8, name="w_scales%d" % l, align_bytes=64)
 
         groups = operand_groups()
         loaded = set()
@@ -114,11 +122,9 @@ def tile_so3_linear_pa_t_kernel(tc, x, W0, W1, W2, W3, bias, out):
             kind, a, b = group
             if kind == "w":
                 nc.sync.dma_start(
-                    out=w_raw[a][:, b * GROUP * C_IN : (b + 1) * GROUP * C_IN].rearrange("p (t m) -> p t m", t=GROUP),
-                    in_=weights[a][b * W_HALF : (b + 1) * W_HALF, :].rearrange("(t p) m -> p t m", p=P),
+                    out=w_raw[a][:, b * GROUP * C_IN : (b + 1) * GROUP * C_IN],
+                    in_=weights[a][b * W_HALF : (b + 1) * W_HALF, :].rearrange("(p j) m -> p (j m)", j=GROUP),
                 )
-                if (a, b) == (0, 0):
-                    nc.sync.dma_start(out=bias_bf16[:], in_=bias.partition_broadcast(P))
                 return
             for l, i in UNITS[b * GROUP : (b + 1) * GROUP]:
                 if (a, l) not in loaded:
@@ -130,8 +136,6 @@ def tile_so3_linear_pa_t_kernel(tc, x, W0, W1, W2, W3, bias, out):
             kind, a, b = group
             if kind == "w":
                 source_words[group] = w_raw[a][:].bitcast(F32)[:, b * GROUP * WORDS : (b + 1) * GROUP * WORDS]
-                if (a, b) == (0, 0):
-                    nc.vector.tensor_copy(out=bias_f32[:], in_=bias_bf16[:])
                 return
             rows = gathered_pool.tile([P, GROUP * C_IN], BF16, name="rows")
             for j in range(GROUP):
@@ -146,17 +150,26 @@ def tile_so3_linear_pa_t_kernel(tc, x, W0, W1, W2, W3, bias, out):
         def flip(group):
             words = source_words[group]
             packed = regrouped_pool.tile([P, GROUP * P * 4], BF16, name="packed", align_bytes=64)
-            packed_words = packed[:].bitcast(F32).rearrange("p (j r u) -> p j r u", j=GROUP, u=2)
             for pair in range(GROUP // 2):
                 flipped = flipped_pool.tile([P, 2, 2, P], F32, name="flipped")
                 for j in range(2):
                     for u in range(2):
                         start = ((2 * pair + j) * 2 + u) * P
                         nc.tensor.transpose(flipped[:, j, u, :], words[:, start : start + P], identity[:])
-                nc.scalar.copy(
-                    out=packed_words[:, 2 * pair : 2 * pair + 2, :, :],
-                    in_=flipped[:].rearrange("p j u r -> p j r u"),
-                )
+                if group[0] == "w":
+                    nc.scalar.copy(
+                        out=packed[:].bitcast(F32).rearrange("p (r j u) -> p r j u", j=GROUP, u=2)[
+                            :, :, 2 * pair : 2 * pair + 2, :
+                        ],
+                        in_=flipped[:].rearrange("p j u r -> p r j u"),
+                    )
+                else:
+                    nc.scalar.copy(
+                        out=packed[:].bitcast(F32).rearrange("p (j r u) -> p j r u", j=GROUP, u=2)[
+                            :, 2 * pair : 2 * pair + 2, :, :
+                        ],
+                        in_=flipped[:].rearrange("p j u r -> p j r u"),
+                    )
             regrouped[group] = packed
 
         def quantise(group):
@@ -169,7 +182,7 @@ def tile_so3_linear_pa_t_kernel(tc, x, W0, W1, W2, W3, bias, out):
             quantised.add(group)
 
         def advance(step):
-            for stage, index in ((quantise, step), (gather, step + 2), (flip, step + 1), (load, step + LOAD_LEAD)):
+            for stage, index in ((quantise, step), (gather, step + 2), (flip, step + 1)):
                 if 0 <= index < len(groups):
                     stage(groups[index])
 
@@ -177,34 +190,33 @@ def tile_so3_linear_pa_t_kernel(tc, x, W0, W1, W2, W3, bias, out):
             assert all(group in quantised for group in operands(bt, l, first_bank, banks))
             d = 2 * l + 1
             width = pass_width(d)
-            moving = max(width, MIN_MOVING)
             staged = staged_pool.tile([P, CHUNK_BANKS * BANK], F32, name="staged")
             for k in range(banks):
                 n0 = (first_bank + k) * width
-                product = product_pool.tile([P, BANK], F32, name="product")
+                product = product_pool.tile([P, d, width], F32, name="product")
                 for i in range(d):
                     unit = first_unit(l) + i
                     nc.tensor.matmul_mx(
-                        out=product[:, i * width : i * width + moving],
+                        out=product[:, i, :],
                         lhsT=x_codes[bt][:, unit * P : (unit + 1) * P].bitcast(FP8X4),
                         lhsT_scale=x_scales[bt][:, unit * P : (unit + 1) * P],
-                        rhs=w_codes[l][:, n0 : n0 + moving].bitcast(FP8X4),
-                        rhs_scale=w_scales[l][:, n0 : n0 + moving],
+                        rhs=w_codes[l][:, n0 : n0 + width].bitcast(FP8X4),
+                        rhs_scale=w_scales[l][:, n0 : n0 + width],
                         start=True,
                         stop=True,
                     )
                 target = staged[:, k * width * d : (k + 1) * width * d]
                 if l == 0:
                     nc.vector.tensor_tensor(
-                        out=target, in0=product[:], in1=bias_f32[:, n0 : n0 + width], op=mybir.AluOpType.add
+                        out=target, in0=product[:, 0, :], in1=bias_f32[:, n0 : n0 + width], op=mybir.AluOpType.add
                     )
                 elif k == 0:
                     nc.vector.tensor_copy(
-                        out=target.rearrange("p (n i) -> p n i", i=d), in_=product[:, : d * width].rearrange("p (i n) -> p n i", i=d)
+                        out=target.rearrange("p (n i) -> p n i", i=d), in_=product[:].rearrange("p i n -> p n i")
                     )
                 else:
                     nc.scalar.copy(
-                        out=target.rearrange("p (n i) -> p n i", i=d), in_=product[:, : d * width].rearrange("p (i n) -> p n i", i=d)
+                        out=target.rearrange("p (n i) -> p n i", i=d), in_=product[:].rearrange("p i n -> p n i")
                     )
             start = C_OUT * l * l + first_bank * width * d
             nc.sync.dma_start(
@@ -213,13 +225,21 @@ def tile_so3_linear_pa_t_kernel(tc, x, W0, W1, W2, W3, bias, out):
             )
 
         chunks = product_chunks()
-        step = -LOAD_LEAD
-        for q in range(-1, len(chunks)):
-            if q >= 0:
-                chunk(*chunks[q])
-                advance(step)
-                step += 1
-            ahead = chunks[min(q + 2, len(chunks) - 1)]
-            while not all(group in quantised for group in operands(*ahead)):
+
+        def ready(number):
+            return all(group in quantised for group in operands(*chunks[min(number, len(chunks) - 1)]))
+
+        for group in groups:
+            load(group)
+        step = -2
+        while not ready(1):
+            advance(step)
+            step += 1
+        spread_bias()
+        for q in range(len(chunks)):
+            chunk(*chunks[q])
+            advance(step)
+            step += 1
+            while not ready(q + 2):
                 advance(step)
                 step += 1

@@ -135,17 +135,23 @@ def tile_so3_linear_pa_t_kernel(tc, x, W0, W1, W2, W3, bias, out):
         def gather(group):
             kind, a, b = group
             if kind == "w":
-                source_words[group] = w_raw[a][:].bitcast(F32)[:, b * GROUP * WORDS : (b + 1) * GROUP * WORDS]
+                words = w_raw[a][:].bitcast(F32)[:, b * GROUP * WORDS : (b + 1) * GROUP * WORDS]
+                source_words[group] = [words[:, j * WORDS : (j + 1) * WORDS] for j in range(GROUP)]
                 return
+            units = UNITS[b * GROUP : (b + 1) * GROUP]
             rows = gathered_pool.tile([P, GROUP * C_IN], BF16, name="rows")
-            for j in range(GROUP):
-                l, i = UNITS[b * GROUP + j]
+            source_words[group] = [rows[:].bitcast(F32)[:, j * WORDS : (j + 1) * WORDS] for j in range(GROUP)]
+            for l in sorted(set(l for l, i in units)):
+                places = [j for j in range(GROUP) if units[j][0] == l]
                 segment = x_raw[a][:, C_IN * l * l : C_IN * (l + 1) * (l + 1)]
+                if l == 0:
+                    source_words[group][places[0]] = segment.bitcast(F32)
+                    continue
+                first, count = units[places[0]][1], len(places)
                 nc.vector.tensor_copy(
-                    out=rows[:, j * C_IN : (j + 1) * C_IN],
-                    in_=segment.rearrange("p (m i) -> p i m", i=2 * l + 1)[:, i, :],
+                    out=rows[:, places[0] * C_IN : (places[0] + count) * C_IN].rearrange("p (i m) -> p m i", i=count),
+                    in_=segment.rearrange("p (m i) -> p m i", i=2 * l + 1)[:, :, first : first + count],
                 )
-            source_words[group] = rows[:].bitcast(F32)
 
         def flip(group):
             words = source_words[group]
@@ -154,8 +160,9 @@ def tile_so3_linear_pa_t_kernel(tc, x, W0, W1, W2, W3, bias, out):
                 flipped = flipped_pool.tile([P, 2, 2, P], F32, name="flipped")
                 for j in range(2):
                     for u in range(2):
-                        start = ((2 * pair + j) * 2 + u) * P
-                        nc.tensor.transpose(flipped[:, j, u, :], words[:, start : start + P], identity[:])
+                        nc.tensor.transpose(
+                            flipped[:, j, u, :], words[2 * pair + j][:, u * P : (u + 1) * P], identity[:]
+                        )
                 if group[0] == "w":
                     nc.scalar.copy(
                         out=packed[:].bitcast(F32).rearrange("p (r j u) -> p r j u", j=GROUP, u=2)[

@@ -71,7 +71,7 @@ def tile_so3_linear_pa_t_kernel(tc, x, W0, W1, W2, W3, bias, out):
 
     with ExitStack() as ctx:
         keep = ctx.enter_context(tc.tile_pool(name="keep", bufs=1))
-        gathered_pool = ctx.enter_context(tc.tile_pool(name="gathered", bufs=3))
+        gathered_pool = ctx.enter_context(tc.tile_pool(name="gathered", bufs=4))
         regrouped_pool = ctx.enter_context(tc.tile_pool(name="regrouped", bufs=3))
         staged_pool = ctx.enter_context(tc.tile_pool(name="staged", bufs=8))
         flipped_pool = ctx.enter_context(tc.psum_pool(name="flipped", bufs=3))
@@ -127,9 +127,10 @@ def tile_so3_linear_pa_t_kernel(tc, x, W0, W1, W2, W3, bias, out):
                 )
                 return
             for l, i in UNITS[b * GROUP : (b + 1) * GROUP]:
-                if (a, l) not in loaded:
-                    loaded.add((a, l))
-                    columns = slice(C_IN * l * l, C_IN * (l + 1) * (l + 1))
+                first, last = (0, 3) if a > 0 else (0, 1) if l < 2 else (l, l)
+                if (a, first) not in loaded:
+                    loaded.add((a, first))
+                    columns = slice(C_IN * first * first, C_IN * (last + 1) * (last + 1))
                     nc.sync.dma_start(out=x_raw[a][:, columns], in_=x[a * P : (a + 1) * P, columns])
 
         def gather(group):
@@ -189,7 +190,7 @@ def tile_so3_linear_pa_t_kernel(tc, x, W0, W1, W2, W3, bias, out):
             quantised.add(group)
 
         def advance(step):
-            for stage, index in ((quantise, step), (gather, step + 2), (flip, step + 1)):
+            for stage, index in ((quantise, step), (gather, step + 3), (flip, step + 1)):
                 if 0 <= index < len(groups):
                     stage(groups[index])
 
@@ -238,12 +239,14 @@ def tile_so3_linear_pa_t_kernel(tc, x, W0, W1, W2, W3, bias, out):
 
         for group in groups:
             load(group)
-        step = -2
+        first_with_bias = min(q for q in range(len(chunks)) if chunks[q][1] == 0)
+        step = -3
         while not ready(1):
             advance(step)
             step += 1
-        spread_bias()
         for q in range(len(chunks)):
+            if q == first_with_bias:
+                spread_bias()
             chunk(*chunks[q])
             advance(step)
             step += 1

@@ -74,8 +74,8 @@ def tile_so3_linear_pa_t_kernel(tc, x, W0, W1, W2, W3, bias, out):
         gathered_pool = ctx.enter_context(tc.tile_pool(name="gathered", bufs=4))
         regrouped_pool = ctx.enter_context(tc.tile_pool(name="regrouped", bufs=3))
         staged_pool = ctx.enter_context(tc.tile_pool(name="staged", bufs=8))
-        flipped_pool = ctx.enter_context(tc.psum_pool(name="flipped", bufs=3))
-        product_pool = ctx.enter_context(tc.psum_pool(name="product", bufs=5))
+        flipped_pool = ctx.enter_context(tc.psum_pool(name="flipped", bufs=4))
+        product_pool = ctx.enter_context(tc.psum_pool(name="product", bufs=4))
         ctx.enter_context(tc.manual_schedule())
 
         identity = keep.tile([P, P], F32, name="identity")
@@ -127,7 +127,7 @@ def tile_so3_linear_pa_t_kernel(tc, x, W0, W1, W2, W3, bias, out):
                 )
                 return
             for l, i in UNITS[b * GROUP : (b + 1) * GROUP]:
-                first, last = (0, 3) if a > 0 else (0, 1) if l < 2 else (l, l)
+                first, last = (0, 3) if a > 0 else (l, l)
                 if (a, first) not in loaded:
                     loaded.add((a, first))
                     columns = slice(C_IN * first * first, C_IN * (last + 1) * (last + 1))
@@ -218,7 +218,7 @@ def tile_so3_linear_pa_t_kernel(tc, x, W0, W1, W2, W3, bias, out):
                     nc.vector.tensor_tensor(
                         out=target, in0=product[:, 0, :], in1=bias_f32[:, n0 : n0 + width], op=mybir.AluOpType.add
                     )
-                elif k == 0:
+                elif k == 0 or (k == 2 and (bt == B_TILES - 1 or first_bank // CHUNK_BANKS % 2 == 1)):
                     nc.vector.tensor_copy(
                         out=target.rearrange("p (n i) -> p n i", i=d), in_=product[:].rearrange("p i n -> p n i")
                     )
@@ -226,11 +226,14 @@ def tile_so3_linear_pa_t_kernel(tc, x, W0, W1, W2, W3, bias, out):
                     nc.scalar.copy(
                         out=target.rearrange("p (n i) -> p n i", i=d), in_=product[:].rearrange("p i n -> p n i")
                     )
+            stores = 2 if (bt, l, first_bank, banks) == chunks[-1] else 1
+            share = banks * width * d // stores
             start = C_OUT * l * l + first_bank * width * d
-            nc.sync.dma_start(
-                out=out[bt * P : (bt + 1) * P, start : start + banks * width * d],
-                in_=staged[:, : banks * width * d],
-            )
+            for part in range(stores):
+                nc.sync.dma_start(
+                    out=out[bt * P : (bt + 1) * P, start + part * share : start + (part + 1) * share],
+                    in_=staged[:, part * share : (part + 1) * share],
+                )
 
         chunks = product_chunks()
 

@@ -105,12 +105,12 @@ def tile_so3_linear_pa_t_kernel(tc, x, W0, W1, W2, W3, bias, out):
 
         x_codes, x_scales = [], []
         for bt in range(B_TILES):
-            x_codes.append(keep.tile([P, len(UNITS) * P], U32, name="x_codes%d" % bt, align_bytes=64))
-            x_scales.append(keep.tile([P, len(UNITS) * P], U8, name="x_scales%d" % bt, align_bytes=64))
+            x_codes.append(keep.tile([P, len(UNITS) * P], U32, name="x_codes%d" % bt, align_bytes=256))
+            x_scales.append(keep.tile([P, len(UNITS) * P], U8, name="x_scales%d" % bt, align_bytes=256))
         w_codes, w_scales = {}, {}
         for l in DEGREES:
-            w_codes[l] = keep.tile([P, C_OUT], U32, name="w_codes%d" % l, align_bytes=64)
-            w_scales[l] = keep.tile([P, C_OUT], U8, name="w_scales%d" % l, align_bytes=64)
+            w_codes[l] = keep.tile([P, C_OUT], U32, name="w_codes%d" % l, align_bytes=256)
+            w_scales[l] = keep.tile([P, C_OUT], U8, name="w_scales%d" % l, align_bytes=256)
 
         groups = operand_groups()
         loaded = set()

from contextlib import ExitStack

import concourse.mybir as mybir
from concourse.masks import make_identity

F32 = mybir.dt.float32
BF16 = mybir.dt.bfloat16
U32 = mybir.dt.uint32
U8 = mybir.dt.uint8
FP8X4 = mybir.dt.float8_e4m3fn_x4

P = 128
BATCH = 384
B_TILES = BATCH // P
C_IN = 512
C_OUT = 1024
WORDS = C_IN // 2
BANK = 512
DEGREES = (1, 0, 3, 2)
UNITS = [(l, i) for l in DEGREES for i in range(2 * l + 1)]
GROUP = 4
W_HALF = GROUP * P
CHUNK_BANKS = 4

FLOPS = 2 * BATCH * len(UNITS) * C_IN * C_OUT


def pass_width(d):
    return max(n for n in (64, 128, 256, 512) if n * d <= BANK)


def first_unit(l):
    return UNITS.index((l, 0))


def operand_groups():
    groups = []
    for bt in range(B_TILES):
        listed = 0
        for l in DEGREES:
            last_group = (first_unit(l) + 2 * l) // GROUP
            while listed <= last_group:
                groups.append(("x", bt, listed))
                listed += 1
            if bt == 0:
                groups.append(("w", l, 0))
                groups.append(("w", l, 1))
    return groups


def product_chunks():
    chunks = []
    for bt in range(B_TILES):
        for l in DEGREES:
            all_banks = C_OUT // pass_width(2 * l + 1)
            banks = min(CHUNK_BANKS, all_banks)
            for first_bank in range(0, all_banks, banks):
                chunks.append((bt, l, first_bank, banks))
    return chunks


def operands(bt, l, first_bank, banks):
    width = pass_width(2 * l + 1)
    halves = [("w", l, (first_bank + k) * width // W_HALF) for k in range(banks)]
    return halves + [("x", bt, (first_unit(l) + i) // GROUP) for i in range(2 * l + 1)]


def tile_so3_linear_pa_t_kernel(tc, x, W0, W1, W2, W3, bias, out):
    nc = tc.nc
    weights = (W0, W1, W2, W3)

    with ExitStack() as ctx:
        keep = ctx.enter_context(tc.tile_pool(name="keep", bufs=1))
        gathered_pool = ctx.enter_context(tc.tile_pool(name="gathered", bufs=4))
        regrouped_pool = ctx.enter_context(tc.tile_pool(name="regrouped", bufs=3))
        staged_pool = ctx.enter_context(tc.tile_pool(name="staged", bufs=8))
        flipped_pool = ctx.enter_context(tc.psum_pool(name="flipped", bufs=4))
        product_pool = ctx.enter_context(tc.psum_pool(name="product", bufs=4))
        ctx.enter_context(tc.manual_schedule())

        identity = keep.tile([P, P], F32, name="identity")
        make_identity(nc, identity[:])

        x_raw = []
        for bt in range(B_TILES):
            x_raw.append(keep.tile([P, x.shape[1]], BF16, name="x_raw%d" % bt))
        w_raw = {}
        for l in DEGREES:
            w_raw[l] = keep.tile([P, 2 * GROUP * C_IN], BF16, name="w_raw%d" % l)

        bias_row = keep.tile([P, C_OUT], BF16, name="bias_row")
        ones = keep.tile([P, P], BF16, name="ones")
        bias_f32 = keep.tile([P, C_OUT], F32, name="bias_f32")
        nc.vector.memset(bias_row[:], 0.0)
        nc.vector.memset(ones[:], 1.0)
        nc.scalar.dma_start(out=bias_row[0:1, :], in_=bias.unsqueeze(0))

        def spread_bias():
            for half in range(C_OUT // BANK):
                spread = product_pool.tile([P, BANK], F32, name="product")
                nc.tensor.matmul(
                    out=spread[:], lhsT=ones[:], rhs=bias_row[:, half * BANK : (half + 1) * BANK], start=True, stop=True
                )
                nc.scalar.copy(out=bias_f32[:, half * BANK : (half + 1) * BANK], in_=spread[:])

        x_codes, x_scales = [], []
        for bt in range(B_TILES):
            x_codes.append(keep.tile([P, len(UNITS) * P], U32, name="x_codes%d" % bt, align_bytes=256))
            x_scales.append(keep.tile([P, len(UNITS) * P], U8, name="x_scales%d" % bt, align_bytes=256))
        w_codes, w_scales = {}, {}
        for l in DEGREES:
            w_codes[l] = keep.tile([P, C_OUT], U32, name="w_codes%d" % l, align_bytes=256)
            w_scales[l] = keep.tile([P, C_OUT], U8, name="w_scales%d" % l, align_bytes=256)

        groups = operand_groups()
        loaded = set()
        source_words = {}
        regrouped = {}
        quantised = set()

        def load(group):
            kind, a, b = group
            if kind == "w":
                nc.sync.dma_start(
                    out=w_raw[a][:, b * GROUP * C_IN : (b + 1) * GROUP * C_IN],
                    in_=weights[a][b * W_HALF : (b + 1) * W_HALF, :].rearrange("(p j) m -> p (j m)", j=GROUP),
                )
                return
            for l, i in UNITS[b * GROUP : (b + 1) * GROUP]:
                first, last = (0, 3) if a > 0 else (l, l)
                if (a, first) not in loaded:
                    loaded.add((a, first))
                    columns = slice(C_IN * first * first, C_IN * (last + 1) * (last + 1))
                    nc.sync.dma_start(out=x_raw[a][:, columns], in_=x[a * P : (a + 1) * P, columns])

        def gather(group):
            kind, a, b = group
            if kind == "w":
                words = w_raw[a][:].bitcast(F32)[:, b * GROUP * WORDS : (b + 1) * GROUP * WORDS]
                source_words[group] = [words[:, j * WORDS : (j + 1) * WORDS] for j in range(GROUP)]
                return
            units = UNITS[b * GROUP : (b + 1) * GROUP]
            rows = gathered_pool.tile([P, GROUP * C_IN], BF16, name="rows")
            source_words[group] = [rows[:].bitcast(F32)[:, j * WORDS : (j + 1) * WORDS] for j in range(GROUP)]
            for l in sorted(set(l for l, i in units)):
                places = [j for j in range(GROUP) if units[j][0] == l]
                segment = x_raw[a][:, C_IN * l * l : C_IN * (l + 1) * (l + 1)]
                if l == 0:
                    source_words[group][places[0]] = segment.bitcast(F32)
                    continue
                first, count = units[places[0]][1], len(places)
                nc.vector.tensor_copy(
                    out=rows[:, places[0] * C_IN : (places[0] + count) * C_IN].rearrange("p (i m) -> p m i", i=count),
                    in_=segment.rearrange("p (m i) -> p m i", i=2 * l + 1)[:, :, first : first + count],
                )

        def flip(group):
            words = source_words[group]
            packed = regrouped_pool.tile([P, GROUP * P * 4], BF16, name="packed", align_bytes=64)
            for pair in range(GROUP // 2):
                flipped = flipped_pool.tile([P, 2, 2, P], F32, name="flipped")
                for j in range(2):
                    for u in range(2):
                        nc.tensor.transpose(
                            flipped[:, j, u, :], words[2 * pair + j][:, u * P : (u + 1) * P], identity[:]
                        )
                if group[0] == "w":
                    nc.scalar.copy(
                        out=packed[:].bitcast(F32).rearrange("p (r j u) -> p r j u", j=GROUP, u=2)[
                            :, :, 2 * pair : 2 * pair + 2, :
                        ],
                        in_=flipped[:].rearrange("p j u r -> p r j u"),
                    )
                else:
                    nc.scalar.copy(
                        out=packed[:].bitcast(F32).rearrange("p (j r u) -> p j r u", j=GROUP, u=2)[
                            :, 2 * pair : 2 * pair + 2, :, :
                        ],
                        in_=flipped[:].rearrange("p j u r -> p j r u"),
                    )
            regrouped[group] = packed

        def quantise(group):
            kind, a, b = group
            codes, scales = (w_codes[a], w_scales[a]) if kind == "w" else (x_codes[a], x_scales[a])
            columns = slice(b * GROUP * P, (b + 1) * GROUP * P)
            nc.vector.quantize_mx(
                out=codes[:, columns].bitcast(FP8X4), scales=scales[:, columns], in_=regrouped[group][:]
            )
            quantised.add(group)

        def advance(step):
            for stage, index in ((quantise, step), (gather, step + 3), (flip, step + 1)):
                if 0 <= index < len(groups):
                    stage(groups[index])

        def chunk(bt, l, first_bank, banks):
            assert all(group in quantised for group in operands(bt, l, first_bank, banks))
            d = 2 * l + 1
            width = pass_width(d)
            staged = staged_pool.tile([P, CHUNK_BANKS * BANK], F32, name="staged")
            for k in range(banks):
                n0 = (first_bank + k) * width
                product = product_pool.tile([P, d, width], F32, name="product")
                for i in range(d):
                    unit = first_unit(l) + i
                    nc.tensor.matmul_mx(
                        out=product[:, i, :],
                        lhsT=x_codes[bt][:, unit * P : (unit + 1) * P].bitcast(FP8X4),
                        lhsT_scale=x_scales[bt][:, unit * P : (unit + 1) * P],
                        rhs=w_codes[l][:, n0 : n0 + width].bitcast(FP8X4),
                        rhs_scale=w_scales[l][:, n0 : n0 + width],
                        start=True,
                        stop=True,
                    )
                target = staged[:, k * width * d : (k + 1) * width * d]
                if l == 0:
                    nc.vector.tensor_tensor(
                        out=target, in0=product[:, 0, :], in1=bias_f32[:, n0 : n0 + width], op=mybir.AluOpType.add
                    )
                elif k == 0 or (k == 2 and (bt == B_TILES - 1 or first_bank // CHUNK_BANKS % 2 == 1)):
                    nc.vector.tensor_copy(
                        out=target.rearrange("p (n i) -> p n i", i=d), in_=product[:].rearrange("p i n -> p n i")
                    )
                else:
                    nc.scalar.copy(
                        out=target.rearrange("p (n i) -> p n i", i=d), in_=product[:].rearrange("p i n -> p n i")
                    )
            stores = 2 if (bt, l, first_bank, banks) == chunks[-1] else 1
            share = banks * width * d // stores
            start = C_OUT * l * l + first_bank * width * d
            for part in range(stores):
                nc.sync.dma_start(
                    out=out[bt * P : (bt + 1) * P, start + part * share : start + (part + 1) * share],
                    in_=staged[:, part * share : (part + 1) * share],
                )

        chunks = product_chunks()

        def ready(number):
            return all(group in quantised for group in operands(*chunks[min(number, len(chunks) - 1)]))

        for group in groups:
            load(group)
        first_with_bias = min(q for q in range(len(chunks)) if chunks[q][1] == 0)
        step = -3
        while not ready(1):
            advance(step)
            step += 1
        for q in range(len(chunks)):
            if q == first_with_bias:
                spread_bias()
            chunk(*chunks[q])
            advance(step)
            step += 1
            while not ready(q + 2):
                advance(step)
                step += 1
